import numpy as np
import ml_dtypes


def mxq(x, axis, fmt="e4m3"):
    dtype, down = {"e4m3": (ml_dtypes.float8_e4m3fn, 7), "e5m2": (ml_dtypes.float8_e5m2, 14)}[fmt]
    v = np.moveaxis(np.asarray(x, np.float32).astype(ml_dtypes.bfloat16).astype(np.float64), axis, -1)
    blocks = v.reshape(v.shape[:-1] + (-1, 32))
    amax = np.abs(blocks).max(-1, keepdims=True)
    byte = np.maximum(np.where(amax > 0, np.frexp(amax)[1] - 1 + 127, 0) - down, 1)
    scale = np.exp2(byte - 127.0)
    codes = (blocks / scale).astype(np.float32).astype(dtype).astype(np.float64)
    return np.moveaxis((codes * scale).reshape(v.shape), -1, axis)


WIDE = False


def mx_kscale(k):
    if not WIDE:
        return np.ones(k)
    levels = np.array([10, -10, 5, -5, 0])
    a = np.random.permutation(np.resize(levels, k // 512 * 4)).reshape(k // 512, 4)
    idx = np.arange(k)
    return np.exp2(a[idx // 512, idx % 128 // 32])


BF16 = ml_dtypes.bfloat16


def bf(x):
    return np.asarray(x, np.float32).astype(BF16)


def f64(x):
    return np.asarray(x).astype(np.float64)


B, EN_MID, DE_MID = 1024, 2048, 4096
K1 = EN_MID // 2
K2 = DE_MID // 2


def setup_inputs():
    s = mx_kscale(K1)
    in_data = np.random.standard_normal((B, K1, 2)) * s[None, :, None]
    return {"in_data": bf(in_data.reshape(B, EN_MID)),
            "W": bf(np.random.standard_normal((DE_MID, K1)) / np.sqrt(K1) / s[None, :]),
            "bias": bf(np.random.standard_normal(DE_MID) * 0.25)}


def reference(in_data, W, bias):
    Bsz = in_data.shape[0]
    x_imag = f64(in_data).reshape(Bsz, K1, 2)[:, :, 1]
    tmp = mxq(x_imag, 1, "e4m3") @ mxq(f64(W), 1, "e4m3").T
    act = np.maximum(tmp + f64(bias), 0.0)
    out_r = act[:, :K2] - act[:, K2:]
    out = np.stack([out_r, np.zeros_like(out_r)], axis=2)
    return out.reshape(Bsz, DE_MID, 1)

@@ -1,0 +1,277 @@
+from contextlib import ExitStack
+
+import concourse.mybir as mybir
+from concourse.masks import make_identity
+
+F32 = mybir.dt.float32
+BF16 = mybir.dt.bfloat16
+U32 = mybir.dt.uint32
+U8 = mybir.dt.uint8
+FP8X4 = mybir.dt.float8_e4m3fn_x4
+ALU = mybir.AluOpType
+
+P = 128
+B = 1024
+K = 1024
+HALF = 2048
+N_CHUNK = B // P
+N_J = 8
+FLOPS = 2 * B * K * 2 * HALF
+
+
+def tile_middlelayer_kernel(tc, in_data, W, bias, out):
+    nc = tc.nc
+    out2d = out.rearrange("b j o -> b (j o)")
+    out_view = out2d.rearrange("(c bb p) w -> c p bb w", c=2, bb=4, p=P)
+
+    with ExitStack() as ctx:
+        const = ctx.enter_context(tc.tile_pool(name="const", bufs=1))
+        io = ctx.enter_context(tc.tile_pool(name="io", bufs=8))
+        wraw = ctx.enter_context(tc.tile_pool(name="wraw", bufs=1))
+        stage = ctx.enter_context(tc.tile_pool(name="stage", bufs=3))
+        codes = ctx.enter_context(tc.tile_pool(name="codes", bufs=1))
+        epi = ctx.enter_context(tc.tile_pool(name="epi", bufs=4))
+        psum = ctx.enter_context(tc.psum_pool(name="psum", bufs=1))
+        ctx.enter_context(tc.manual_schedule())
+
+        ident = const.tile([P, P], F32, name="ident")
+        make_identity(nc, ident[:])
+        zeros = const.tile([P, 256], BF16, name="zeros")
+        nc.vector.memset(zeros[:], 0.0)
+        bias_rows = const.tile([P, 256], F32, name="bias_rows")
+        nc.vector.memset(bias_rows[:], 0.0)
+
+        bias_raw = const.tile([16, 256], BF16, name="bias_raw")
+        nc.scalar.dma_start(out=bias_raw[:], in_=bias.rearrange("(r q) -> r q", q=256))
+
+        x_in = {}
+        w_in = {}
+
+        def load_x_pair(pair):
+            t = io.tile([P, 2, 2 * K], BF16, name="xin%d" % pair, tag="io")
+            for i in range(2):
+                bb = 2 * pair + i
+                nc.sync.dma_start(out=t[:, i, :], in_=in_data[bb * P : (bb + 1) * P, :])
+                x_in[bb] = t[:, i, :]
+
+        def load_w(J, h):
+            t = wraw.tile([P, 2 * K], BF16, name="w%d_%d" % (J, h))
+            row0 = h * HALF + J * 256
+            nc.sync.dma_start(
+                out=t[:], in_=W[row0 : row0 + 256, :].rearrange("(n s) k -> n (s k)", s=2)
+            )
+            w_in[(J, h)] = t
+
+        units = [(J, h) for J in range(N_J) for h in (1, 0)]
+        load_x_pair(0)
+        load_x_pair(1)
+        for unit in units[0:4]:
+            load_w(*unit)
+        load_x_pair(2)
+        load_x_pair(3)
+        for unit in units[4:]:
+            load_w(*unit)
+
+        bank_count = [0]
+
+        def next_bank():
+            i = bank_count[0] % 4
+            bank_count[0] += 1
+            return psum.tile([P, 512], F32, name="m%d" % i, tag="m%d" % i)
+
+        r_bank = []
+        for bb in range(4):
+            t = psum.tile([P, 512], F32, name="rb%d" % bb, tag="rb%d" % bb)
+            nc.tensor.matmul(
+                out=t[:, 256:512], lhsT=zeros[:, 0:P], rhs=zeros[:, 0:256], start=True, stop=True
+            )
+            r_bank.append(t)
+
+        nc.vector.tensor_copy(
+            out=bias_rows[0:16, :].rearrange("r (s n) -> r s n", s=2),
+            in_=bias_raw[0:16, :].rearrange("r (n s) -> r s n", s=2),
+        )
+        bias_t = next_bank()
+        for s in range(2):
+            nc.tensor.transpose(
+                bias_t[:, s * P : (s + 1) * P], bias_rows[:, s * P : (s + 1) * P], ident[:]
+            )
+        bias_sb = const.tile([P, 2, 16], F32, name="bias_sb")
+        neg_b1 = const.tile([P, 2, 8], F32, name="neg_b1")
+        delta = const.tile([P, 2, 8], F32, name="delta")
+
+        def bias_scalars():
+            nc.vector.tensor_copy(
+                out=bias_sb[:],
+                in_=bias_t[:, 0:256].rearrange("p (s r) -> p s r", s=2)[:, :, 0:16],
+            )
+            nc.vector.tensor_scalar(
+                out=neg_b1[:], in0=bias_sb[:, :, 0:8], scalar1=-1.0, scalar2=None, op0=ALU.mult
+            )
+            nc.vector.tensor_tensor(
+                out=delta[:], in0=bias_sb[:, :, 8:16], in1=bias_sb[:, :, 0:8], op=ALU.subtract
+            )
+
+        x_codes = codes.tile([P, 2, B], U32, name="x_codes", align_bytes=64)
+        x_scales = codes.tile([P, 2, B], U8, name="x_scales", align_bytes=64)
+        w_codes = {}
+        w_scales = {}
+        for J, h in units:
+            w_codes[(J, h)] = codes.tile([P, 512], U32, name="wc%d_%d" % (J, h), align_bytes=64)
+            w_scales[(J, h)] = codes.tile([P, 512], U8, name="ws%d_%d" % (J, h), align_bytes=64)
+
+        x_compact = {}
+        x_grouped = {}
+
+        def x_compaction(bb, engine):
+            t = stage.tile([P, K], BF16, name="xcmp", tag="xcmp", bufs=4)
+            src = x_in[bb].rearrange("p (k two) -> p k two", two=2)[:, :, 1]
+            if engine == "vector":
+                nc.vector.tensor_copy(out=t[:], in_=src)
+            else:
+                nc.gpsimd.tensor_scalar(
+                    out=t[:], in0=src, scalar1=1.0, scalar2=0.0,
+                    op0=ALU.mult, op1=ALU.add,
+                )
+            x_compact[bb] = t
+
+        def x_transposes(bb):
+            words = x_compact[bb][:].bitcast(F32)
+            bank = next_bank()
+            for q in range(4):
+                nc.tensor.transpose(
+                    bank[:, q * P : (q + 1) * P], words[:, q * P : (q + 1) * P], ident[:]
+                )
+            g_tile = stage.tile([P, K], BF16, name="xg", tag="xg", align_bytes=64)
+            nc.scalar.copy(
+                out=g_tile[:].bitcast(F32).rearrange("p (g b u) -> p g b u", g=2, u=2),
+                in_=bank[:].rearrange("p (g u b) -> p g b u", g=2, u=2),
+            )
+            x_grouped[bb] = g_tile
+
+        def x_quantise(bb):
+            for g in range(2):
+                nc.vector.quantize_mx(
+                    out=x_codes[:, g, bb * P : (bb + 1) * P].bitcast(FP8X4),
+                    scales=x_scales[:, g, bb * P : (bb + 1) * P],
+                    in_=x_grouped[bb][:, g * 512 : (g + 1) * 512],
+                )
+
+        w_grouped = {}
+
+        def w_transposes(unit):
+            words = w_in[unit][:].bitcast(F32)
+            g_tile = stage.tile([P, 2 * K], BF16, name="wg", tag="wg", align_bytes=64)
+            g_words = g_tile[:].bitcast(F32)
+            for s in range(2):
+                bank = next_bank()
+                for q in range(4):
+                    lo = s * 512 + q * P
+                    nc.tensor.transpose(bank[:, q * P : (q + 1) * P], words[:, lo : lo + P], ident[:])
+                nc.scalar.copy(
+                    out=g_words[:, s * 512 : (s + 1) * 512].rearrange(
+                        "p (g n u) -> p g n u", g=2, u=2
+                    ),
+                    in_=bank[:].rearrange("p (g u n) -> p g n u", g=2, u=2),
+                )
+            w_grouped[unit] = g_tile
+
+        def w_quantise(unit):
+            nc.vector.quantize_mx(
+                out=w_codes[unit][:].bitcast(FP8X4), scales=w_scales[unit][:], in_=w_grouped[unit][:]
+            )
+
+        def mx_and_fold(J, c):
+            r_tiles = []
+            for s in range(2):
+                acc = {}
+                for h in (1, 0):
+                    acc[h] = next_bank()
+                    for g in range(2):
+                        lo = s * 256 + g * P
+                        nc.tensor.matmul_mx(
+                            out=acc[h][:],
+                            lhsT=w_codes[(J, h)][:, lo : lo + P].bitcast(FP8X4),
+                            lhsT_scale=w_scales[(J, h)][:, lo : lo + P],
+                            rhs=x_codes[:, g, c * 512 : (c + 1) * 512].bitcast(FP8X4),
+                            rhs_scale=x_scales[:, g, c * 512 : (c + 1) * 512],
+                            start=(g == 0),
+                            stop=(g == 1),
+                        )
+                d2 = epi.tile([P, 512], F32, name="d2", tag="d2")
+                nc.vector.tensor_scalar(
+                    out=d2[:], in0=acc[1][:],
+                    scalar1=delta[:, s, J : J + 1], scalar2=neg_b1[:, s, J : J + 1],
+                    op0=ALU.add, op1=ALU.max,
+                )
+                r = epi.tile([P, 512], F32, name="r", tag="r")
+                nc.vector.scalar_tensor_tensor(
+                    out=r[:], in0=acc[0][:], scalar=neg_b1[:, s, J : J + 1], in1=d2[:],
+                    op0=ALU.max, op1=ALU.subtract,
+                )
+                r_tiles.append(r)
+            return r_tiles
+
+        def r_transposes(r_tiles):
+            for s in range(2):
+                for bb in range(4):
+                    nc.tensor.transpose(
+                        r_bank[bb][:, s * P : (s + 1) * P],
+                        r_tiles[s][:, bb * P : (bb + 1) * P],
+                        ident[:],
+                    )
+
+        def copy_out_and_store(J, c, split_store):
+            o = io.tile([P, 4, 512], F32, name="o", tag="io")
+            for bb in range(4):
+                src = r_bank[bb][:].rearrange("p (e s n) -> p n s e", e=2, s=2)
+                dst = o[:, bb, :].rearrange("p (n s e) -> p n s e", s=2, e=2)
+                if bb == 3:
+                    nc.vector.tensor_copy(out=dst, in_=src)
+                else:
+                    nc.scalar.copy(out=dst, in_=src)
+                if split_store:
+                    nc.sync.dma_start(
+                        out=out_view[c][:, bb, J * 512 : (J + 1) * 512], in_=o[:, bb, :]
+                    )
+            if not split_store:
+                nc.sync.dma_start(out=out_view[c][:, :, J * 512 : (J + 1) * 512], in_=o[:])
+
+        x_compaction(0, "vector")
+        x_compaction(1, "vector")
+        bias_scalars()
+        x_transposes(0)
+        x_compaction(2, "vector")
+        x_transposes(1)
+        x_quantise(0)
+        x_compaction(3, "vector")
+        x_transposes(2)
+        x_quantise(1)
+        x_transposes(3)
+        x_quantise(2)
+        x_quantise(3)
+        for i in range(4):
+            w_transposes(units[i])
+            if i > 0:
+                w_quantise(units[i - 1])
+        w_quantise(units[3])
+        for bb in range(4, 8):
+            x_compaction(bb, "gpsimd")
+
+        rounds = [(0, 0), (1, 0), (0, 1), (1, 1)] + [(J, c) for J in range(2, N_J) for c in range(2)]
+        pending = None
+        for i, (J, c) in enumerate(rounds):
+            r_tiles = mx_and_fold(J, c)
+            unit = units[4 + i] if 4 + i < len(units) else None
+            if unit is not None:
+                w_transposes(unit)
+            late_x = [4 + 2 * i, 5 + 2 * i] if i < 2 else []
+            for bb in late_x:
+                x_transposes(bb)
+            r_transposes(r_tiles)
+            if pending is not None:
+                w_quantise(pending)
+            pending = unit
+            for bb in late_x:
+                x_quantise(bb)
+            copy_out_and_store(J, c, split_store=(i == len(rounds) - 1))

@@ -213,20 +213,20 @@ def tile_middlelayer_kernel(tc, in_data, W, bias, out):
             return r_tiles
 
         def r_transposes(r_tiles):
-            for s in range(2):
-                for bb in range(4):
+            for bb in range(4):
+                for s in range(2):
                     nc.tensor.transpose(
                         r_bank[bb][:, s * P : (s + 1) * P],
                         r_tiles[s][:, bb * P : (bb + 1) * P],
                         ident[:],
                     )
 
-        def copy_out_and_store(J, c, split_store):
+        def copy_out_and_store(J, c, vector_blocks, split_store):
             o = io.tile([P, 4, 512], F32, name="o", tag="io")
             for bb in range(4):
                 src = r_bank[bb][:].rearrange("p (e s n) -> p n s e", e=2, s=2)
                 dst = o[:, bb, :].rearrange("p (n s e) -> p n s e", s=2, e=2)
-                if bb == 3:
+                if bb in vector_blocks:
                     nc.vector.tensor_copy(out=dst, in_=src)
                 else:
                     nc.scalar.copy(out=dst, in_=src)
@@ -260,18 +260,32 @@ def tile_middlelayer_kernel(tc, in_data, W, bias, out):
 
         rounds = [(0, 0), (1, 0), (0, 1), (1, 1)] + [(J, c) for J in range(2, N_J) for c in range(2)]
         pending = None
-        for i, (J, c) in enumerate(rounds):
-            r_tiles = mx_and_fold(J, c)
-            unit = units[4 + i] if 4 + i < len(units) else None
-            if unit is not None:
-                w_transposes(unit)
-            late_x = [4 + 2 * i, 5 + 2 * i] if i < 2 else []
-            for bb in late_x:
-                x_transposes(bb)
-            r_transposes(r_tiles)
+        n_rounds = len(rounds)
+        folded = {}
+        for i in range(n_rounds + 2):
+            if i >= 2:
+                J, c = rounds[i - 2]
+                if i - 2 == n_rounds - 1:
+                    copy_out_and_store(J, c, vector_blocks=(1, 3), split_store=True)
+                else:
+                    copy_out_and_store(
+                        J, c, vector_blocks=((3,) if (i % 2 == 1 or i == n_rounds) else ()), split_store=False
+                    )
+            unit = None
+            late_x = []
+            if i < n_rounds:
+                J, c = rounds[i]
+                folded[i] = mx_and_fold(J, c)
+                unit = units[4 + i] if 4 + i < len(units) else None
+                if unit is not None:
+                    w_transposes(unit)
+                late_x = [4 + 2 * i, 5 + 2 * i] if i < 2 else []
+                for bb in late_x:
+                    x_transposes(bb)
+            if 1 <= i <= n_rounds:
+                r_transposes(folded[i - 1])
             if pending is not None:
                 w_quantise(pending)
             pending = unit
             for bb in late_x:
                 x_quantise(bb)
-            copy_out_and_store(J, c, split_store=(i == len(rounds) - 1))

@@ -181,36 +181,33 @@ def tile_middlelayer_kernel(tc, in_data, W, bias, out):
                 out=w_codes[unit][:].bitcast(FP8X4), scales=w_scales[unit][:], in_=w_grouped[unit][:]
             )
 
-        def mx_and_fold(J, c):
-            r_tiles = []
-            for s in range(2):
-                acc = {}
-                for h in (1, 0):
-                    acc[h] = next_bank()
-                    for g in range(2):
-                        lo = s * 256 + g * P
-                        nc.tensor.matmul_mx(
-                            out=acc[h][:],
-                            lhsT=w_codes[(J, h)][:, lo : lo + P].bitcast(FP8X4),
-                            lhsT_scale=w_scales[(J, h)][:, lo : lo + P],
-                            rhs=x_codes[:, g, c * 512 : (c + 1) * 512].bitcast(FP8X4),
-                            rhs_scale=x_scales[:, g, c * 512 : (c + 1) * 512],
-                            start=(g == 0),
-                            stop=(g == 1),
-                        )
-                d2 = epi.tile([P, 512], F32, name="d2", tag="d2")
-                nc.vector.tensor_scalar(
-                    out=d2[:], in0=acc[1][:],
-                    scalar1=delta[:, s, J : J + 1], scalar2=neg_b1[:, s, J : J + 1],
-                    op0=ALU.add, op1=ALU.max,
-                )
-                r = epi.tile([P, 512], F32, name="r", tag="r")
-                nc.vector.scalar_tensor_tensor(
-                    out=r[:], in0=acc[0][:], scalar=neg_b1[:, s, J : J + 1], in1=d2[:],
-                    op0=ALU.max, op1=ALU.subtract,
-                )
-                r_tiles.append(r)
-            return r_tiles
+        def mx_and_fold(J, c, s):
+            acc = {}
+            for h in (1, 0):
+                acc[h] = next_bank()
+                for g in range(2):
+                    lo = s * 256 + g * P
+                    nc.tensor.matmul_mx(
+                        out=acc[h][:],
+                        lhsT=w_codes[(J, h)][:, lo : lo + P].bitcast(FP8X4),
+                        lhsT_scale=w_scales[(J, h)][:, lo : lo + P],
+                        rhs=x_codes[:, g, c * 512 : (c + 1) * 512].bitcast(FP8X4),
+                        rhs_scale=x_scales[:, g, c * 512 : (c + 1) * 512],
+                        start=(g == 0),
+                        stop=(g == 1),
+                    )
+            d2 = epi.tile([P, 512], F32, name="d2", tag="d2")
+            nc.vector.tensor_scalar(
+                out=d2[:], in0=acc[1][:],
+                scalar1=delta[:, s, J : J + 1], scalar2=neg_b1[:, s, J : J + 1],
+                op0=ALU.add, op1=ALU.max,
+            )
+            r = epi.tile([P, 512], F32, name="r", tag="r")
+            nc.vector.scalar_tensor_tensor(
+                out=r[:], in0=acc[0][:], scalar=neg_b1[:, s, J : J + 1], in1=d2[:],
+                op0=ALU.max, op1=ALU.subtract,
+            )
+            return r
 
         def r_transposes(r_tiles):
             for bb in range(4):
@@ -262,30 +259,31 @@ def tile_middlelayer_kernel(tc, in_data, W, bias, out):
         pending = None
         n_rounds = len(rounds)
         folded = {}
-        for i in range(n_rounds + 2):
-            if i >= 2:
-                J, c = rounds[i - 2]
-                if i - 2 == n_rounds - 1:
+        for i in range(n_rounds + 1):
+            if i < n_rounds:
+                J, c = rounds[i]
+                folded[i] = [mx_and_fold(J, c, 0)]
+            if pending is not None:
+                w_quantise(pending)
+                pending = None
+            if i >= 1:
+                r_transposes(folded[i - 1])
+                J, c = rounds[i - 1]
+                if i == n_rounds:
                     copy_out_and_store(J, c, vector_blocks=(1, 3), split_store=True)
                 else:
                     copy_out_and_store(
-                        J, c, vector_blocks=((3,) if (i % 2 == 1 or i == n_rounds) else ()), split_store=False
+                        J, c, vector_blocks=((3,) if i % 2 == 1 else ()), split_store=False
                     )
-            unit = None
-            late_x = []
             if i < n_rounds:
                 J, c = rounds[i]
-                folded[i] = mx_and_fold(J, c)
+                folded[i].append(mx_and_fold(J, c, 1))
                 unit = units[4 + i] if 4 + i < len(units) else None
                 if unit is not None:
                     w_transposes(unit)
+                pending = unit
                 late_x = [4 + 2 * i, 5 + 2 * i] if i < 2 else []
                 for bb in late_x:
                     x_transposes(bb)
-            if 1 <= i <= n_rounds:
-                r_transposes(folded[i - 1])
-            if pending is not None:
-                w_quantise(pending)
-            pending = unit
-            for bb in late_x:
-                x_quantise(bb)
+                for bb in late_x:
+                    x_quantise(bb)

@@ -65,18 +65,14 @@ def tile_middlelayer_kernel(tc, in_data, W, bias, out):
         units = [(J, h) for J in range(N_J) for h in (1, 0)]
         load_x_pair(0)
         load_x_pair(1)
-        for unit in units[0:4]:
+        for unit in units[0:6]:
             load_w(*unit)
         load_x_pair(2)
         load_x_pair(3)
-        for unit in units[4:]:
+        for unit in units[6:]:
             load_w(*unit)
 
-        bank_count = [0]
-
-        def next_bank():
-            i = bank_count[0] % 4
-            bank_count[0] += 1
+        def m_bank(i):
             return psum.tile([P, 512], F32, name="m%d" % i, tag="m%d" % i)
 
         r_bank = []
@@ -91,7 +87,7 @@ def tile_middlelayer_kernel(tc, in_data, W, bias, out):
             out=bias_rows[0:16, :].rearrange("r (s n) -> r s n", s=2),
             in_=bias_raw[0:16, :].rearrange("r (n s) -> r s n", s=2),
         )
-        bias_t = next_bank()
+        bias_t = m_bank(0)
         for s in range(2):
             nc.tensor.transpose(
                 bias_t[:, s * P : (s + 1) * P], bias_rows[:, s * P : (s + 1) * P], ident[:]
@@ -135,9 +131,9 @@ def tile_middlelayer_kernel(tc, in_data, W, bias, out):
                 )
             x_compact[bb] = t
 
-        def x_transposes(bb):
+        def x_transposes(bb, bank_index):
             words = x_compact[bb][:].bitcast(F32)
-            bank = next_bank()
+            bank = m_bank(bank_index)
             for q in range(4):
                 nc.tensor.transpose(
                     bank[:, q * P : (q + 1) * P], words[:, q * P : (q + 1) * P], ident[:]
@@ -159,12 +155,12 @@ def tile_middlelayer_kernel(tc, in_data, W, bias, out):
 
         w_grouped = {}
 
-        def w_transposes(unit):
+        def w_transposes(unit, bank_indices):
             words = w_in[unit][:].bitcast(F32)
             g_tile = stage.tile([P, 2 * K], BF16, name="wg", tag="wg", align_bytes=64)
             g_words = g_tile[:].bitcast(F32)
             for s in range(2):
-                bank = next_bank()
+                bank = m_bank(bank_indices[s])
                 for q in range(4):
                     lo = s * 512 + q * P
                     nc.tensor.transpose(bank[:, q * P : (q + 1) * P], words[:, lo : lo + P], ident[:])
@@ -181,10 +177,10 @@ def tile_middlelayer_kernel(tc, in_data, W, bias, out):
                 out=w_codes[unit][:].bitcast(FP8X4), scales=w_scales[unit][:], in_=w_grouped[unit][:]
             )
 
-        def mx_and_fold(J, c, s):
+        def mx_and_fold(J, c, s, bank_indices):
             acc = {}
             for h in (1, 0):
-                acc[h] = next_bank()
+                acc[h] = m_bank(bank_indices[1 - h])
                 for g in range(2):
                     lo = s * 256 + g * P
                     nc.tensor.matmul_mx(
@@ -218,9 +214,9 @@ def tile_middlelayer_kernel(tc, in_data, W, bias, out):
                         ident[:],
                     )
 
-        def copy_out_and_store(J, c, vector_blocks, split_store):
+        def copy_out_and_store(J, c, block_order, vector_blocks, split_store):
             o = io.tile([P, 4, 512], F32, name="o", tag="io")
-            for bb in range(4):
+            for bb in block_order:
                 src = r_bank[bb][:].rearrange("p (e s n) -> p n s e", e=2, s=2)
                 dst = o[:, bb, :].rearrange("p (n s e) -> p n s e", s=2, e=2)
                 if bb in vector_blocks:
@@ -237,53 +233,77 @@ def tile_middlelayer_kernel(tc, in_data, W, bias, out):
         x_compaction(0, "vector")
         x_compaction(1, "vector")
         bias_scalars()
-        x_transposes(0)
+        x_transposes(0, 1)
         x_compaction(2, "vector")
-        x_transposes(1)
+        x_transposes(1, 2)
         x_quantise(0)
         x_compaction(3, "vector")
-        x_transposes(2)
+        x_transposes(2, 3)
         x_quantise(1)
-        x_transposes(3)
+        x_transposes(3, 0)
         x_quantise(2)
         x_quantise(3)
         for i in range(4):
-            w_transposes(units[i])
+            w_transposes(units[i], ((1, 2), (3, 0))[i % 2])
             if i > 0:
                 w_quantise(units[i - 1])
         w_quantise(units[3])
         for bb in range(4, 8):
             x_compaction(bb, "gpsimd")
 
-        rounds = [(0, 0), (1, 0), (0, 1), (1, 1)] + [(J, c) for J in range(2, N_J) for c in range(2)]
-        pending = None
+        rounds = [(J, c) for c in range(2) for J in range(3)]
+        rounds += [(J, c) for J in range(3, N_J) for c in range(2)]
         n_rounds = len(rounds)
+        w_after = {0: [units[4], units[5]]}
+        for i in range(2, 12):
+            w_after[i] = [units[4 + i]]
+        x_after = {1: [4, 5], 2: [6, 7]}
+
+        banks = [1, 2, 3, 0]
+        pending = []
         folded = {}
         for i in range(n_rounds + 1):
+            last = i == n_rounds - 1
+            if 2 <= i < n_rounds:
+                J, c = rounds[i - 2]
+                copy_out_and_store(
+                    J, c, block_order=(0, 1, 2, 3),
+                    vector_blocks=(), split_store=False,
+                )
+            regrouped = []
+            late_x = []
             if i < n_rounds:
                 J, c = rounds[i]
-                folded[i] = [mx_and_fold(J, c, 0)]
-            if pending is not None:
-                w_quantise(pending)
-                pending = None
-            if i >= 1:
+                folded[i] = [mx_and_fold(J, c, 0, banks[0:2])]
+                if last:
+                    r_transposes(folded[i - 1])
+                    J1, c1 = rounds[i - 1]
+                    copy_out_and_store(
+                        J1, c1, block_order=(0, 1, 2, 3), vector_blocks=(), split_store=False
+                    )
+                folded[i].append(mx_and_fold(J, c, 1, banks[2:4]))
+                a0, a1, a2, a3 = banks
+                free = [a0, a1, a2, a3]
+                regrouped = w_after.get(i, [])
+                late_x = x_after.get(i, [])
+                for unit in regrouped:
+                    w_transposes(unit, (free[0], free[1]))
+                    free = free[2:]
+                for bb in late_x:
+                    x_transposes(bb, free[0])
+                    free = free[1:]
+                if len(free) == 2:
+                    banks = [a2, a3, a0, a1]
+            if i >= 1 and i < n_rounds - 1:
+                r_transposes(folded[i - 1])
+            if i == n_rounds:
                 r_transposes(folded[i - 1])
                 J, c = rounds[i - 1]
-                if i == n_rounds:
-                    copy_out_and_store(J, c, vector_blocks=(1, 3), split_store=True)
-                else:
-                    copy_out_and_store(
-                        J, c, vector_blocks=((3,) if i % 2 == 1 else ()), split_store=False
-                    )
-            if i < n_rounds:
-                J, c = rounds[i]
-                folded[i].append(mx_and_fold(J, c, 1))
-                unit = units[4 + i] if 4 + i < len(units) else None
-                if unit is not None:
-                    w_transposes(unit)
-                pending = unit
-                late_x = [4 + 2 * i, 5 + 2 * i] if i < 2 else []
-                for bb in late_x:
-                    x_transposes(bb)
-                for bb in late_x:
-                    x_quantise(bb)
+                copy_out_and_store(
+                    J, c, block_order=(0, 1, 2, 3), vector_blocks=(1, 3), split_store=True
+                )
+            for unit in pending:
+                w_quantise(unit)
+            pending = regrouped
+            for bb in late_x:
+                x_quantise(bb)

@@ -14,9 +14,11 @@ P = 128
 B = 1024
 K = 1024
 HALF = 2048
-N_CHUNK = B // P
 N_J = 8
 FLOPS = 2 * B * K * 2 * HALF
+WG_BUFS = 10
+HEAD_ENGINES = ("scalar", "vector", "scalar", "vector")
+EARLY_JOBS = (0, 1, 2)
 
 
 def tile_middlelayer_kernel(tc, in_data, W, bias, out):
@@ -54,25 +56,34 @@ def tile_middlelayer_kernel(tc, in_data, W, bias, out):
                 nc.sync.dma_start(out=t[:, i, :], in_=in_data[bb * P : (bb + 1) * P, :])
                 x_in[bb] = t[:, i, :]
 
-        def load_w(J, h):
-            t = wraw.tile([P, 2 * K], BF16, name="w%d_%d" % (J, h))
-            row0 = h * HALF + J * 256
-            nc.sync.dma_start(
-                out=t[:], in_=W[row0 : row0 + 256, :].rearrange("(n s) k -> n (s k)", s=2)
-            )
-            w_in[(J, h)] = t
+        def w_tile(J, h):
+            if (J, h) not in w_in:
+                w_in[(J, h)] = wraw.tile([P, 2, K], BF16, name="w%d_%d" % (J, h))
+            return w_in[(J, h)]
 
-        units = [(J, h) for J in range(N_J) for h in (1, 0)]
+        def w_rows(J, h):
+            row0 = h * HALF + J * 256
+            return W[row0 : row0 + 256, :].rearrange("(n s) k -> n s k", s=2)
+
+        def load_w(J, h):
+            nc.sync.dma_start(out=w_tile(J, h)[:], in_=w_rows(J, h))
+
         load_x_pair(0)
         load_x_pair(1)
-        for unit in units[0:6]:
-            load_w(*unit)
+        for J in (0, 1, 2):
+            for h in (1, 0):
+                load_w(J, h)
         load_x_pair(2)
         load_x_pair(3)
-        for unit in units[6:]:
-            load_w(*unit)
+        for J in range(3, N_J):
+            for h in (1, 0):
+                load_w(J, h)
 
-        def m_bank(i):
+        bank_count = [0]
+
+        def next_bank():
+            i = bank_count[0] % 4
+            bank_count[0] += 1
             return psum.tile([P, 512], F32, name="m%d" % i, tag="m%d" % i)
 
         r_bank = []
@@ -87,7 +98,7 @@ def tile_middlelayer_kernel(tc, in_data, W, bias, out):
             out=bias_rows[0:16, :].rearrange("r (s n) -> r s n", s=2),
             in_=bias_raw[0:16, :].rearrange("r (n s) -> r s n", s=2),
         )
-        bias_t = m_bank(0)
+        bias_t = next_bank()
         for s in range(2):
             nc.tensor.transpose(
                 bias_t[:, s * P : (s + 1) * P], bias_rows[:, s * P : (s + 1) * P], ident[:]
@@ -95,12 +106,11 @@ def tile_middlelayer_kernel(tc, in_data, W, bias, out):
         bias_sb = const.tile([P, 2, 16], F32, name="bias_sb")
         neg_b1 = const.tile([P, 2, 8], F32, name="neg_b1")
         delta = const.tile([P, 2, 8], F32, name="delta")
+        nc.scalar.copy(
+            out=bias_sb[:], in_=bias_t[:, 0:256].rearrange("p (s r) -> p s r", s=2)[:, :, 0:16]
+        )
 
         def bias_scalars():
-            nc.vector.tensor_copy(
-                out=bias_sb[:],
-                in_=bias_t[:, 0:256].rearrange("p (s r) -> p s r", s=2)[:, :, 0:16],
-            )
             nc.vector.tensor_scalar(
                 out=neg_b1[:], in0=bias_sb[:, :, 0:8], scalar1=-1.0, scalar2=None, op0=ALU.mult
             )
@@ -112,9 +122,16 @@ def tile_middlelayer_kernel(tc, in_data, W, bias, out):
         x_scales = codes.tile([P, 2, B], U8, name="x_scales", align_bytes=64)
         w_codes = {}
         w_scales = {}
-        for J, h in units:
-            w_codes[(J, h)] = codes.tile([P, 512], U32, name="wc%d_%d" % (J, h), align_bytes=64)
-            w_scales[(J, h)] = codes.tile([P, 512], U8, name="ws%d_%d" % (J, h), align_bytes=64)
+        for J in range(N_J):
+            for h in range(2):
+                w_codes[(J, h)] = codes.tile([P, 512], U32, name="wc%d_%d" % (J, h), align_bytes=64)
+                w_scales[(J, h)] = codes.tile([P, 512], U8, name="ws%d_%d" % (J, h), align_bytes=64)
+
+        def copy_out(engine, dst, src):
+            if engine == "vector":
+                nc.vector.tensor_copy(out=dst, in_=src)
+            else:
+                nc.scalar.copy(out=dst, in_=src)
 
         x_compact = {}
         x_grouped = {}
@@ -131,17 +148,18 @@ def tile_middlelayer_kernel(tc, in_data, W, bias, out):
                 )
             x_compact[bb] = t
 
-        def x_transposes(bb, bank_index):
+        def x_transposes(bb, engine="scalar"):
             words = x_compact[bb][:].bitcast(F32)
-            bank = m_bank(bank_index)
+            bank = next_bank()
             for q in range(4):
                 nc.tensor.transpose(
                     bank[:, q * P : (q + 1) * P], words[:, q * P : (q + 1) * P], ident[:]
                 )
             g_tile = stage.tile([P, K], BF16, name="xg", tag="xg", align_bytes=64)
-            nc.scalar.copy(
-                out=g_tile[:].bitcast(F32).rearrange("p (g b u) -> p g b u", g=2, u=2),
-                in_=bank[:].rearrange("p (g u b) -> p g b u", g=2, u=2),
+            copy_out(
+                engine,
+                g_tile[:].bitcast(F32).rearrange("p (g b u) -> p g b u", g=2, u=2),
+                bank[:].rearrange("p (g u b) -> p g b u", g=2, u=2),
             )
             x_grouped[bb] = g_tile
 
@@ -155,52 +173,60 @@ def tile_middlelayer_kernel(tc, in_data, W, bias, out):
 
         w_grouped = {}
 
-        def w_transposes(unit, bank_indices):
-            words = w_in[unit][:].bitcast(F32)
-            g_tile = stage.tile([P, 2 * K], BF16, name="wg", tag="wg", align_bytes=64)
-            g_words = g_tile[:].bitcast(F32)
-            for s in range(2):
-                bank = m_bank(bank_indices[s])
-                for q in range(4):
-                    lo = s * 512 + q * P
-                    nc.tensor.transpose(bank[:, q * P : (q + 1) * P], words[:, lo : lo + P], ident[:])
-                nc.scalar.copy(
-                    out=g_words[:, s * 512 : (s + 1) * 512].rearrange(
-                        "p (g n u) -> p g n u", g=2, u=2
-                    ),
-                    in_=bank[:].rearrange("p (g u n) -> p g n u", g=2, u=2),
-                )
-            w_grouped[unit] = g_tile
+        def w_transposes(J, h, s, engine="scalar"):
+            words = w_in[(J, h)][:, s, :].bitcast(F32)
+            g_tile = stage.tile([P, K], BF16, name="wg", tag="wg", bufs=WG_BUFS, align_bytes=64)
+            bank = next_bank()
+            for q in range(4):
+                nc.tensor.transpose(bank[:, q * P : (q + 1) * P], words[:, q * P : (q + 1) * P], ident[:])
+            copy_out(
+                engine,
+                g_tile[:].bitcast(F32).rearrange("p (g n u) -> p g n u", g=2, u=2),
+                bank[:].rearrange("p (g u n) -> p g n u", g=2, u=2),
+            )
+            w_grouped[(J, h, s)] = g_tile
 
-        def w_quantise(unit):
+        def w_quantise(J, h, s):
             nc.vector.quantize_mx(
-                out=w_codes[unit][:].bitcast(FP8X4), scales=w_scales[unit][:], in_=w_grouped[unit][:]
+                out=w_codes[(J, h)][:, s * 256 : (s + 1) * 256].bitcast(FP8X4),
+                scales=w_scales[(J, h)][:, s * 256 : (s + 1) * 256],
+                in_=w_grouped[(J, h, s)][:],
             )
 
-        def mx_and_fold(J, c, s, bank_indices):
-            acc = {}
-            for h in (1, 0):
-                acc[h] = m_bank(bank_indices[1 - h])
-                for g in range(2):
-                    lo = s * 256 + g * P
-                    nc.tensor.matmul_mx(
-                        out=acc[h][:],
-                        lhsT=w_codes[(J, h)][:, lo : lo + P].bitcast(FP8X4),
-                        lhsT_scale=w_scales[(J, h)][:, lo : lo + P],
-                        rhs=x_codes[:, g, c * 512 : (c + 1) * 512].bitcast(FP8X4),
-                        rhs_scale=x_scales[:, g, c * 512 : (c + 1) * 512],
-                        start=(g == 0),
-                        stop=(g == 1),
-                    )
+        def quantise(job):
+            if job[0] == "x":
+                x_quantise(job[1])
+            else:
+                w_quantise(job[1], job[2], job[3])
+
+        def mx(J, c, s, h):
+            acc = next_bank()
+            for g in range(2):
+                lo = s * 256 + g * P
+                nc.tensor.matmul_mx(
+                    out=acc[:],
+                    lhsT=w_codes[(J, h)][:, lo : lo + P].bitcast(FP8X4),
+                    lhsT_scale=w_scales[(J, h)][:, lo : lo + P],
+                    rhs=x_codes[:, g, c * 512 : (c + 1) * 512].bitcast(FP8X4),
+                    rhs_scale=x_scales[:, g, c * 512 : (c + 1) * 512],
+                    start=(g == 0),
+                    stop=(g == 1),
+                )
+            return acc
+
+        def fold_first(J, s, acc):
             d2 = epi.tile([P, 512], F32, name="d2", tag="d2")
             nc.vector.tensor_scalar(
-                out=d2[:], in0=acc[1][:],
+                out=d2[:], in0=acc[:],
                 scalar1=delta[:, s, J : J + 1], scalar2=neg_b1[:, s, J : J + 1],
                 op0=ALU.add, op1=ALU.max,
             )
+            return d2
+
+        def fold_second(J, s, acc, d2):
             r = epi.tile([P, 512], F32, name="r", tag="r")
             nc.vector.scalar_tensor_tensor(
-                out=r[:], in0=acc[0][:], scalar=neg_b1[:, s, J : J + 1], in1=d2[:],
+                out=r[:], in0=acc[:], scalar=neg_b1[:, s, J : J + 1], in1=d2[:],
                 op0=ALU.max, op1=ALU.subtract,
             )
             return r
@@ -214,15 +240,14 @@ def tile_middlelayer_kernel(tc, in_data, W, bias, out):
                         ident[:],
                     )
 
-        def copy_out_and_store(J, c, block_order, vector_blocks, split_store):
+        def copy_out_and_store(J, c, vector_blocks, split_store):
             o = io.tile([P, 4, 512], F32, name="o", tag="io")
-            for bb in block_order:
-                src = r_bank[bb][:].rearrange("p (e s n) -> p n s e", e=2, s=2)
-                dst = o[:, bb, :].rearrange("p (n s e) -> p n s e", s=2, e=2)
-                if bb in vector_blocks:
-                    nc.vector.tensor_copy(out=dst, in_=src)
-                else:
-                    nc.scalar.copy(out=dst, in_=src)
+            for bb in range(4):
+                copy_out(
+                    "vector" if bb in vector_blocks else "scalar",
+                    o[:, bb, :].rearrange("p (n s e) -> p n s e", s=2, e=2),
+                    r_bank[bb][:].rearrange("p (e s n) -> p n s e", e=2, s=2),
+                )
                 if split_store:
                     nc.sync.dma_start(
                         out=out_view[c][:, bb, J * 512 : (J + 1) * 512], in_=o[:, bb, :]
@@ -231,79 +256,76 @@ def tile_middlelayer_kernel(tc, in_data, W, bias, out):
                 nc.sync.dma_start(out=out_view[c][:, :, J * 512 : (J + 1) * 512], in_=o[:])
 
         x_compaction(0, "vector")
+        x_transposes(0)
         x_compaction(1, "vector")
-        bias_scalars()
-        x_transposes(0, 1)
+        x_transposes(1)
         x_compaction(2, "vector")
-        x_transposes(1, 2)
         x_quantise(0)
+        x_transposes(2)
         x_compaction(3, "vector")
-        x_transposes(2, 3)
         x_quantise(1)
-        x_transposes(3, 0)
+        x_transposes(3)
         x_quantise(2)
-        x_quantise(3)
-        for i in range(4):
-            w_transposes(units[i], ((1, 2), (3, 0))[i % 2])
-            if i > 0:
-                w_quantise(units[i - 1])
-        w_quantise(units[3])
+        bias_scalars()
+        head_w = [(0, 1, 0), (0, 1, 1), (0, 0, 0), (0, 0, 1)]
+        for i, (J, h, s) in enumerate(head_w):
+            w_transposes(J, h, s, HEAD_ENGINES[i])
+            if i == 0:
+                x_quantise(3)
+            if i >= 1:
+                w_quantise(*head_w[i - 1])
+        w_quantise(*head_w[3])
         for bb in range(4, 8):
             x_compaction(bb, "gpsimd")
 
         rounds = [(J, c) for c in range(2) for J in range(3)]
         rounds += [(J, c) for J in range(3, N_J) for c in range(2)]
         n_rounds = len(rounds)
-        w_after = {0: [units[4], units[5]]}
+        halves = [(J, h, s) for J in range(3, N_J) for h in (1, 0) for s in range(2)]
+        w_after = {0: [(J, h, s) for J in (1, 2) for h in (1, 0) for s in range(2)]}
         for i in range(2, 12):
-            w_after[i] = [units[4 + i]]
+            w_after[i] = halves[2 * (i - 2) : 2 * (i - 1)]
         x_after = {1: [4, 5], 2: [6, 7]}
 
-        banks = [1, 2, 3, 0]
-        pending = []
+        jobs = []
         folded = {}
         for i in range(n_rounds + 1):
             last = i == n_rounds - 1
             if 2 <= i < n_rounds:
                 J, c = rounds[i - 2]
-                copy_out_and_store(
-                    J, c, block_order=(0, 1, 2, 3),
-                    vector_blocks=(), split_store=False,
-                )
-            regrouped = []
-            late_x = []
+                copy_out_and_store(J, c, vector_blocks=(), split_store=False)
             if i < n_rounds:
                 J, c = rounds[i]
-                folded[i] = [mx_and_fold(J, c, 0, banks[0:2])]
+                acc = {}
+                acc[(0, 1)] = mx(J, c, 0, 1)
+                acc[(1, 1)] = mx(J, c, 1, 1)
                 if last:
                     r_transposes(folded[i - 1])
                     J1, c1 = rounds[i - 1]
-                    copy_out_and_store(
-                        J1, c1, block_order=(0, 1, 2, 3), vector_blocks=(), split_store=False
-                    )
-                folded[i].append(mx_and_fold(J, c, 1, banks[2:4]))
-                a0, a1, a2, a3 = banks
-                free = [a0, a1, a2, a3]
-                regrouped = w_after.get(i, [])
-                late_x = x_after.get(i, [])
-                for unit in regrouped:
-                    w_transposes(unit, (free[0], free[1]))
-                    free = free[2:]
-                for bb in late_x:
-                    x_transposes(bb, free[0])
-                    free = free[1:]
-                if len(free) == 2:
-                    banks = [a2, a3, a0, a1]
+                    copy_out_and_store(J1, c1, vector_blocks=(), split_store=False)
+                acc[(0, 0)] = mx(J, c, 0, 0)
+                acc[(1, 0)] = mx(J, c, 1, 0)
+                d20 = fold_first(J, 0, acc[(0, 1)])
+                d21 = fold_first(J, 1, acc[(1, 1)])
+                r0 = fold_second(J, 0, acc[(0, 0)], d20)
+                r1 = fold_second(J, 1, acc[(1, 0)], d21)
+                for job in jobs:
+                    quantise(job)
+                folded[i] = [r0, r1]
+                jobs = []
+                for k, (Jw, h, s) in enumerate(w_after.get(i, [])):
+                    w_transposes(Jw, h, s, "scalar")
+                    jobs.append(("w", Jw, h, s))
+                for bb in x_after.get(i, []):
+                    x_transposes(bb)
+                    jobs.append(("x", bb))
+                if i in EARLY_JOBS:
+                    for job in jobs:
+                        quantise(job)
+                    jobs = []
             if i >= 1 and i < n_rounds - 1:
                 r_transposes(folded[i - 1])
             if i == n_rounds:
                 r_transposes(folded[i - 1])
                 J, c = rounds[i - 1]
-                copy_out_and_store(
-                    J, c, block_order=(0, 1, 2, 3), vector_blocks=(1, 3), split_store=True
-                )
-            for unit in pending:
-                w_quantise(unit)
-            pending = regrouped
-            for bb in late_x:
-                x_quantise(bb)
+                copy_out_and_store(J, c, vector_blocks=(1, 3), split_store=True)

@@ -14,9 +14,14 @@ P = 128
 B = 1024
 K = 1024
 HALF = 2048
-N_J = 8
+N_J = 4
+N_D = 2
+J_SPLIT = N_J * 256
 FLOPS = 2 * B * K * 2 * HALF
 WG_BUFS = 10
+W_BUFS = 10
+T_BUFS = 6
+RELU_ENGINES = ("scalar", "scalar")
 HEAD_ENGINES = ("scalar", "vector", "scalar", "vector")
 EARLY_JOBS = (0, 1, 2)
 
@@ -28,8 +33,8 @@ def tile_middlelayer_kernel(tc, in_data, W, bias, out):
 
     with ExitStack() as ctx:
         const = ctx.enter_context(tc.tile_pool(name="const", bufs=1))
-        io = ctx.enter_context(tc.tile_pool(name="io", bufs=8))
-        wraw = ctx.enter_context(tc.tile_pool(name="wraw", bufs=1))
+        io = ctx.enter_context(tc.tile_pool(name="io", bufs=6))
+        wraw = ctx.enter_context(tc.tile_pool(name="wraw", bufs=W_BUFS))
         stage = ctx.enter_context(tc.tile_pool(name="stage", bufs=3))
         codes = ctx.enter_context(tc.tile_pool(name="codes", bufs=1))
         epi = ctx.enter_context(tc.tile_pool(name="epi", bufs=4))
@@ -42,6 +47,12 @@ def tile_middlelayer_kernel(tc, in_data, W, bias, out):
         nc.vector.memset(zeros[:], 0.0)
         bias_rows = const.tile([P, 256], F32, name="bias_rows")
         nc.vector.memset(bias_rows[:], 0.0)
+
+        wide_out = []
+        for i in range(4):
+            t = const.tile([P, 512, 2], F32, name="wide_out%d" % i)
+            nc.vector.memset(t[:], 0.0)
+            wide_out.append(t)
 
         bias_raw = const.tile([16, 256], BF16, name="bias_raw")
         nc.scalar.dma_start(out=bias_raw[:], in_=bias.rearrange("(r q) -> r q", q=256))
@@ -56,28 +67,38 @@ def tile_middlelayer_kernel(tc, in_data, W, bias, out):
                 nc.sync.dma_start(out=t[:, i, :], in_=in_data[bb * P : (bb + 1) * P, :])
                 x_in[bb] = t[:, i, :]
 
-        def w_tile(J, h):
-            if (J, h) not in w_in:
-                w_in[(J, h)] = wraw.tile([P, 2, K], BF16, name="w%d_%d" % (J, h))
-            return w_in[(J, h)]
+        def load_w(unit):
+            t = wraw.tile([P, 2, K], BF16, name="w", tag="w")
+            if unit[0] == "R":
+                row0 = unit[2] * HALF + unit[1] * 256
+                rows = W[row0 : row0 + 256, :].rearrange("(n s) k -> n s k", s=2)
+            else:
+                row0 = unit[2] * HALF + J_SPLIT + unit[1] * 512 + unit[3] * 256
+                rows = W[row0 : row0 + 256, :].rearrange("(s n) k -> n s k", s=2)
+            nc.sync.dma_start(out=t[:], in_=rows)
+            w_in[unit] = t
 
-        def w_rows(J, h):
-            row0 = h * HALF + J * 256
-            return W[row0 : row0 + 256, :].rearrange("(n s) k -> n s k", s=2)
+        def r_units(J):
+            return [("R", J, 1), ("R", J, 0)]
 
-        def load_w(J, h):
-            nc.sync.dma_start(out=w_tile(J, h)[:], in_=w_rows(J, h))
+        def b_units(D):
+            return [("B", D, h, m) for h in (1, 0) for m in range(2)]
 
+        units = r_units(0) + r_units(1) + b_units(0) + r_units(2) + b_units(1) + r_units(3)
+        bias_wide = const.tile([P, 2, N_D * 512], BF16, name="bias_wide")
         load_x_pair(0)
         load_x_pair(1)
-        for J in (0, 1, 2):
-            for h in (1, 0):
-                load_w(J, h)
+        for unit in units[0:8]:
+            load_w(unit)
+        for h in range(2):
+            lo = h * HALF + J_SPLIT
+            nc.sync.dma_start(
+                out=bias_wide[:, h, :], in_=bias[lo : lo + N_D * 512].partition_broadcast(P)
+            )
         load_x_pair(2)
         load_x_pair(3)
-        for J in range(3, N_J):
-            for h in (1, 0):
-                load_w(J, h)
+        for unit in units[8:]:
+            load_w(unit)
 
         bank_count = [0]
 
@@ -126,6 +147,16 @@ def tile_middlelayer_kernel(tc, in_data, W, bias, out):
             for h in range(2):
                 w_codes[(J, h)] = codes.tile([P, 512], U32, name="wc%d_%d" % (J, h), align_bytes=64)
                 w_scales[(J, h)] = codes.tile([P, 512], U8, name="ws%d_%d" % (J, h), align_bytes=64)
+        wide_codes = {}
+        wide_scales = {}
+        for D in range(N_D):
+            for h in range(2):
+                wide_codes[(D, h)] = codes.tile(
+                    [P, 2, 512], U32, name="vc%d_%d" % (D, h), align_bytes=64
+                )
+                wide_scales[(D, h)] = codes.tile(
+                    [P, 2, 512], U8, name="vs%d_%d" % (D, h), align_bytes=64
+                )
 
         def copy_out(engine, dst, src):
             if engine == "vector":
@@ -173,8 +204,8 @@ def tile_middlelayer_kernel(tc, in_data, W, bias, out):
 
         w_grouped = {}
 
-        def w_transposes(J, h, s, engine="scalar"):
-            words = w_in[(J, h)][:, s, :].bitcast(F32)
+        def w_transposes(unit, s, engine="scalar"):
+            words = w_in[unit][:, s, :].bitcast(F32)
             g_tile = stage.tile([P, K], BF16, name="wg", tag="wg", bufs=WG_BUFS, align_bytes=64)
             bank = next_bank()
             for q in range(4):
@@ -184,20 +215,31 @@ def tile_middlelayer_kernel(tc, in_data, W, bias, out):
                 g_tile[:].bitcast(F32).rearrange("p (g n u) -> p g n u", g=2, u=2),
                 bank[:].rearrange("p (g u n) -> p g n u", g=2, u=2),
             )
-            w_grouped[(J, h, s)] = g_tile
+            w_grouped[(unit, s)] = g_tile
 
-        def w_quantise(J, h, s):
-            nc.vector.quantize_mx(
-                out=w_codes[(J, h)][:, s * 256 : (s + 1) * 256].bitcast(FP8X4),
-                scales=w_scales[(J, h)][:, s * 256 : (s + 1) * 256],
-                in_=w_grouped[(J, h, s)][:],
-            )
+        def w_quantise(unit, s):
+            if unit[0] == "R":
+                key = (unit[1], unit[2])
+                nc.vector.quantize_mx(
+                    out=w_codes[key][:, s * 256 : (s + 1) * 256].bitcast(FP8X4),
+                    scales=w_scales[key][:, s * 256 : (s + 1) * 256],
+                    in_=w_grouped[(unit, s)][:],
+                )
+            else:
+                key = (unit[1], unit[2])
+                lo = unit[3] * 256 + s * P
+                for g in range(2):
+                    nc.vector.quantize_mx(
+                        out=wide_codes[key][:, g, lo : lo + P].bitcast(FP8X4),
+                        scales=wide_scales[key][:, g, lo : lo + P],
+                        in_=w_grouped[(unit, s)][:, g * 512 : (g + 1) * 512],
+                    )
 
         def quantise(job):
             if job[0] == "x":
                 x_quantise(job[1])
             else:
-                w_quantise(job[1], job[2], job[3])
+                w_quantise(job[1], job[2])
 
         def mx(J, c, s, h):
             acc = next_bank()
@@ -230,6 +272,47 @@ def tile_middlelayer_kernel(tc, in_data, W, bias, out):
                 op0=ALU.max, op1=ALU.subtract,
             )
             return r
+
+        def mx_wide(D, bb, h):
+            acc = next_bank()
+            for g in range(2):
+                nc.tensor.matmul_mx(
+                    out=acc[:],
+                    lhsT=x_codes[:, g, bb * P : (bb + 1) * P].bitcast(FP8X4),
+                    lhsT_scale=x_scales[:, g, bb * P : (bb + 1) * P],
+                    rhs=wide_codes[(D, h)][:, g, :].bitcast(FP8X4),
+                    rhs_scale=wide_scales[(D, h)][:, g, :],
+                    start=(g == 0),
+                    stop=(g == 1),
+                )
+            return acc
+
+        def add_bias(D, h, acc):
+            t = epi.tile([P, 512], F32, name="t", tag="t", bufs=T_BUFS)
+            nc.vector.tensor_tensor(
+                out=t[:], in0=acc[:], in1=bias_wide[:, h, D * 512 : (D + 1) * 512], op=ALU.add
+            )
+            return t
+
+        def relu(t, engine):
+            if engine == "scalar":
+                nc.scalar.activation(out=t[:], in_=t[:], func=mybir.ActivationFunctionType.Relu)
+            else:
+                nc.gpsimd.tensor_scalar(
+                    out=t[:], in0=t[:], scalar1=3.0e38, scalar2=0.0, op0=ALU.min, op1=ALU.max
+                )
+
+        wide_count = [0]
+
+        def subtract_and_store(D, bb, t1, t2):
+            o = wide_out[wide_count[0] % 4]
+            wide_count[0] += 1
+            nc.gpsimd.tensor_tensor(out=o[:, :, 0], in0=t1[:], in1=t2[:], op=ALU.subtract)
+            lo = 2 * (J_SPLIT + D * 512)
+            nc.sync.dma_start(
+                out=out2d[bb * P : (bb + 1) * P, lo : lo + 1024],
+                in_=o[:].rearrange("p j e -> p (j e)"),
+            )
 
         def r_transposes(r_tiles):
             for bb in range(4):
@@ -267,9 +350,9 @@ def tile_middlelayer_kernel(tc, in_data, W, bias, out):
         x_transposes(3)
         x_quantise(2)
         bias_scalars()
-        head_w = [(0, 1, 0), (0, 1, 1), (0, 0, 0), (0, 0, 1)]
-        for i, (J, h, s) in enumerate(head_w):
-            w_transposes(J, h, s, HEAD_ENGINES[i])
+        head_w = [(unit, s) for unit in units[0:2] for s in range(2)]
+        for i, (unit, s) in enumerate(head_w):
+            w_transposes(unit, s, HEAD_ENGINES[i])
             if i == 0:
                 x_quantise(3)
             if i >= 1:
@@ -278,54 +361,72 @@ def tile_middlelayer_kernel(tc, in_data, W, bias, out):
         for bb in range(4, 8):
             x_compaction(bb, "gpsimd")
 
-        rounds = [(J, c) for c in range(2) for J in range(3)]
-        rounds += [(J, c) for J in range(3, N_J) for c in range(2)]
-        n_rounds = len(rounds)
-        halves = [(J, h, s) for J in range(3, N_J) for h in (1, 0) for s in range(2)]
-        w_after = {0: [(J, h, s) for J in (1, 2) for h in (1, 0) for s in range(2)]}
-        for i in range(2, 12):
-            w_after[i] = halves[2 * (i - 2) : 2 * (i - 1)]
-        x_after = {1: [4, 5], 2: [6, 7]}
+        items = [
+            ("R", 0, 0), ("R", 1, 0), ("B", 0, (0, 1)), ("B", 0, (2, 3)),
+            ("R", 0, 1), ("B", 0, (4, 5)), ("R", 1, 1), ("B", 0, (6, 7)),
+            ("R", 2, 0), ("B", 1, (0, 1)), ("R", 3, 0), ("B", 1, (2, 3)),
+            ("R", 2, 1), ("B", 1, (4, 5)), ("B", 1, (6, 7)), ("R", 3, 1),
+        ]
+        n_items = len(items)
+        w_after = {
+            0: units[2:6], 1: units[6:8], 4: units[8:10], 5: units[10:11], 6: units[11:12],
+            7: units[12:14], 8: units[14:16],
+        }
+        x_after = {2: [4, 5, 6, 7]}
 
         jobs = []
-        folded = {}
-        for i in range(n_rounds + 1):
-            last = i == n_rounds - 1
-            if 2 <= i < n_rounds:
-                J, c = rounds[i - 2]
-                copy_out_and_store(J, c, vector_blocks=(), split_store=False)
-            if i < n_rounds:
-                J, c = rounds[i]
+        to_transpose = None
+        to_copy = None
+        for i, item in enumerate(items):
+            last = i == n_items - 1
+            if to_copy is not None:
+                copy_out_and_store(to_copy[0], to_copy[1], vector_blocks=(), split_store=False)
+                to_copy = None
+            fresh = None
+            if item[0] == "R":
+                J, c = item[1], item[2]
                 acc = {}
-                acc[(0, 1)] = mx(J, c, 0, 1)
-                acc[(1, 1)] = mx(J, c, 1, 1)
-                if last:
-                    r_transposes(folded[i - 1])
-                    J1, c1 = rounds[i - 1]
-                    copy_out_and_store(J1, c1, vector_blocks=(), split_store=False)
-                acc[(0, 0)] = mx(J, c, 0, 0)
-                acc[(1, 0)] = mx(J, c, 1, 0)
+                for h in (1, 0):
+                    for s in range(2):
+                        acc[(s, h)] = mx(J, c, s, h)
                 d20 = fold_first(J, 0, acc[(0, 1)])
                 d21 = fold_first(J, 1, acc[(1, 1)])
                 r0 = fold_second(J, 0, acc[(0, 0)], d20)
                 r1 = fold_second(J, 1, acc[(1, 0)], d21)
+                fresh = (J, c, [r0, r1])
+            else:
+                D = item[1]
+                acc = {}
+                for bb in item[2]:
+                    for h in (1, 0):
+                        acc[(bb, h)] = mx_wide(D, bb, h)
+                sums = {}
+                for bb in item[2]:
+                    for h in (1, 0):
+                        sums[(bb, h)] = add_bias(D, h, acc[(bb, h)])
+                for bb in item[2]:
+                    relu(sums[(bb, 1)], RELU_ENGINES[0])
+                    relu(sums[(bb, 0)], RELU_ENGINES[1])
+                    subtract_and_store(D, bb, sums[(bb, 0)], sums[(bb, 1)])
+            for job in jobs:
+                quantise(job)
+            jobs = []
+            for unit in w_after.get(i, []):
+                for s in range(2):
+                    w_transposes(unit, s, "scalar")
+                    jobs.append(("w", unit, s))
+            for bb in x_after.get(i, []):
+                x_transposes(bb)
+                jobs.append(("x", bb))
+            if i in EARLY_JOBS:
                 for job in jobs:
                     quantise(job)
-                folded[i] = [r0, r1]
                 jobs = []
-                for k, (Jw, h, s) in enumerate(w_after.get(i, [])):
-                    w_transposes(Jw, h, s, "scalar")
-                    jobs.append(("w", Jw, h, s))
-                for bb in x_after.get(i, []):
-                    x_transposes(bb)
-                    jobs.append(("x", bb))
-                if i in EARLY_JOBS:
-                    for job in jobs:
-                        quantise(job)
-                    jobs = []
-            if i >= 1 and i < n_rounds - 1:
-                r_transposes(folded[i - 1])
-            if i == n_rounds:
-                r_transposes(folded[i - 1])
-                J, c = rounds[i - 1]
-                copy_out_and_store(J, c, vector_blocks=(1, 3), split_store=True)
+            if to_transpose is not None:
+                r_transposes(to_transpose[2])
+                to_copy = (to_transpose[0], to_transpose[1])
+                to_transpose = None
+            if fresh is not None:
+                to_transpose = fresh
+        r_transposes(to_transpose[2])
+        copy_out_and_store(to_transpose[0], to_transpose[1], vector_blocks=(1, 3), split_store=True)

@@ -23,7 +23,9 @@ W_BUFS = 10
 T_BUFS = 6
 RELU_ENGINES = ("scalar", "scalar")
 HEAD_ENGINES = ("scalar", "vector", "scalar", "vector")
-EARLY_JOBS = (0, 1, 2)
+EARLY_JOBS = (0, 1, 2, 3)
+X_LATE_AFTER = 10
+V_COPY_EVERY = 99
 
 
 def tile_middlelayer_kernel(tc, in_data, W, bias, out):
@@ -84,11 +86,11 @@ def tile_middlelayer_kernel(tc, in_data, W, bias, out):
         def b_units(D):
             return [("B", D, h, m) for h in (1, 0) for m in range(2)]
 
-        units = r_units(0) + r_units(1) + b_units(0) + r_units(2) + b_units(1) + r_units(3)
+        units = r_units(0) + r_units(1) + r_units(2) + r_units(3) + b_units(0) + b_units(1)
         bias_wide = const.tile([P, 2, N_D * 512], BF16, name="bias_wide")
         load_x_pair(0)
         load_x_pair(1)
-        for unit in units[0:8]:
+        for unit in units[0:X_LATE_AFTER]:
             load_w(unit)
         for h in range(2):
             lo = h * HALF + J_SPLIT
@@ -97,7 +99,7 @@ def tile_middlelayer_kernel(tc, in_data, W, bias, out):
             )
         load_x_pair(2)
         load_x_pair(3)
-        for unit in units[8:]:
+        for unit in units[X_LATE_AFTER:]:
             load_w(unit)
 
         bank_count = [0]
@@ -362,17 +364,15 @@ def tile_middlelayer_kernel(tc, in_data, W, bias, out):
             x_compaction(bb, "gpsimd")
 
         items = [
-            ("R", 0, 0), ("R", 1, 0), ("B", 0, (0, 1)), ("B", 0, (2, 3)),
-            ("R", 0, 1), ("B", 0, (4, 5)), ("R", 1, 1), ("B", 0, (6, 7)),
-            ("R", 2, 0), ("B", 1, (0, 1)), ("R", 3, 0), ("B", 1, (2, 3)),
-            ("R", 2, 1), ("B", 1, (4, 5)), ("B", 1, (6, 7)), ("R", 3, 1),
+            ("R", 0, 0), ("R", 1, 0), ("R", 2, 0), ("R", 3, 0),
+            ("B", 0, (0, 1)), ("B", 0, (2, 3)), ("R", 0, 1),
+            ("B", 0, (4, 5)), ("B", 0, (6, 7)), ("R", 1, 1),
+            ("B", 1, (0, 1)), ("B", 1, (2, 3)), ("R", 2, 1),
+            ("B", 1, (4, 5)), ("B", 1, (6, 7)), ("R", 3, 1),
         ]
         n_items = len(items)
-        w_after = {
-            0: units[2:6], 1: units[6:8], 4: units[8:10], 5: units[10:11], 6: units[11:12],
-            7: units[12:14], 8: units[14:16],
-        }
-        x_after = {2: [4, 5, 6, 7]}
+        w_after = {0: units[2:6], 1: units[6:10], 2: units[10:14], 3: units[14:16]}
+        x_after = {3: [4, 5, 6, 7]}
 
         jobs = []
         to_transpose = None
@@ -411,9 +411,9 @@ def tile_middlelayer_kernel(tc, in_data, W, bias, out):
             for job in jobs:
                 quantise(job)
             jobs = []
-            for unit in w_after.get(i, []):
+            for k, unit in enumerate(w_after.get(i, [])):
                 for s in range(2):
-                    w_transposes(unit, s, "scalar")
+                    w_transposes(unit, s, "vector" if (2 * k + s) % V_COPY_EVERY == 1 else "scalar")
                     jobs.append(("w", unit, s))
             for bb in x_after.get(i, []):
                 x_transposes(bb)

from contextlib import ExitStack

import concourse.mybir as mybir
from concourse.masks import make_identity

F32 = mybir.dt.float32
BF16 = mybir.dt.bfloat16
U32 = mybir.dt.uint32
U8 = mybir.dt.uint8
FP8X4 = mybir.dt.float8_e4m3fn_x4
ALU = mybir.AluOpType

P = 128
B = 1024
K = 1024
HALF = 2048
N_J = 4
N_D = 2
J_SPLIT = N_J * 256
FLOPS = 2 * B * K * 2 * HALF
WG_BUFS = 10
W_BUFS = 10
T_BUFS = 6
RELU_ENGINES = ("scalar", "scalar")
HEAD_ENGINES = ("scalar", "vector", "scalar", "vector")
EARLY_JOBS = (0, 1, 2, 3)
X_LATE_AFTER = 10
V_COPY_EVERY = 99


def tile_middlelayer_kernel(tc, in_data, W, bias, out):
    nc = tc.nc
    out2d = out.rearrange("b j o -> b (j o)")
    out_view = out2d.rearrange("(c bb p) w -> c p bb w", c=2, bb=4, p=P)

    with ExitStack() as ctx:
        const = ctx.enter_context(tc.tile_pool(name="const", bufs=1))
        io = ctx.enter_context(tc.tile_pool(name="io", bufs=6))
        wraw = ctx.enter_context(tc.tile_pool(name="wraw", bufs=W_BUFS))
        stage = ctx.enter_context(tc.tile_pool(name="stage", bufs=3))
        codes = ctx.enter_context(tc.tile_pool(name="codes", bufs=1))
        epi = ctx.enter_context(tc.tile_pool(name="epi", bufs=4))
        psum = ctx.enter_context(tc.psum_pool(name="psum", bufs=1))
        ctx.enter_context(tc.manual_schedule())

        ident = const.tile([P, P], F32, name="ident")
        make_identity(nc, ident[:])
        zeros = const.tile([P, 256], BF16, name="zeros")
        nc.vector.memset(zeros[:], 0.0)
        bias_rows = const.tile([P, 256], F32, name="bias_rows")
        nc.vector.memset(bias_rows[:], 0.0)

        wide_out = []
        for i in range(4):
            t = const.tile([P, 512, 2], F32, name="wide_out%d" % i)
            nc.vector.memset(t[:], 0.0)
            wide_out.append(t)

        bias_raw = const.tile([16, 256], BF16, name="bias_raw")
        nc.scalar.dma_start(out=bias_raw[:], in_=bias.rearrange("(r q) -> r q", q=256))

        x_in = {}
        w_in = {}

        def load_x_pair(pair):
            t = io.tile([P, 2, 2 * K], BF16, name="xin%d" % pair, tag="io")
            for i in range(2):
                bb = 2 * pair + i
                nc.sync.dma_start(out=t[:, i, :], in_=in_data[bb * P : (bb + 1) * P, :])
                x_in[bb] = t[:, i, :]

        def load_w(unit):
            t = wraw.tile([P, 2, K], BF16, name="w", tag="w")
            if unit[0] == "R":
                row0 = unit[2] * HALF + unit[1] * 256
                rows = W[row0 : row0 + 256, :].rearrange("(n s) k -> n s k", s=2)
            else:
                row0 = unit[2] * HALF + J_SPLIT + unit[1] * 512 + unit[3] * 256
                rows = W[row0 : row0 + 256, :].rearrange("(s n) k -> n s k", s=2)
            nc.sync.dma_start(out=t[:], in_=rows)
            w_in[unit] = t

        def r_units(J):
            return [("R", J, 1), ("R", J, 0)]

        def b_units(D):
            return [("B", D, h, m) for h in (1, 0) for m in range(2)]

        units = r_units(0) + r_units(1) + r_units(2) + r_units(3) + b_units(0) + b_units(1)
        bias_wide = const.tile([P, 2, N_D * 512], BF16, name="bias_wide")
        load_x_pair(0)
        load_x_pair(1)
        for unit in units[0:X_LATE_AFTER]:
            load_w(unit)
        for h in range(2):
            lo = h * HALF + J_SPLIT
            nc.sync.dma_start(
                out=bias_wide[:, h, :], in_=bias[lo : lo + N_D * 512].partition_broadcast(P)
            )
        load_x_pair(2)
        load_x_pair(3)
        for unit in units[X_LATE_AFTER:]:
            load_w(unit)

        bank_count = [0]

        def next_bank():
            i = bank_count[0] % 4
            bank_count[0] += 1
            return psum.tile([P, 512], F32, name="m%d" % i, tag="m%d" % i)

        r_bank = []
        for bb in range(4):
            t = psum.tile([P, 512], F32, name="rb%d" % bb, tag="rb%d" % bb)
            nc.tensor.matmul(
                out=t[:, 256:512], lhsT=zeros[:, 0:P], rhs=zeros[:, 0:256], start=True, stop=True
            )
            r_bank.append(t)

        nc.vector.tensor_copy(
            out=bias_rows[0:16, :].rearrange("r (s n) -> r s n", s=2),
            in_=bias_raw[0:16, :].rearrange("r (n s) -> r s n", s=2),
        )
        bias_t = next_bank()
        for s in range(2):
            nc.tensor.transpose(
                bias_t[:, s * P : (s + 1) * P], bias_rows[:, s * P : (s + 1) * P], ident[:]
            )
        bias_sb = const.tile([P, 2, 16], F32, name="bias_sb")
        neg_b1 = const.tile([P, 2, 8], F32, name="neg_b1")
        delta = const.tile([P, 2, 8], F32, name="delta")
        nc.scalar.copy(
            out=bias_sb[:], in_=bias_t[:, 0:256].rearrange("p (s r) -> p s r", s=2)[:, :, 0:16]
        )

        def bias_scalars():
            nc.vector.tensor_scalar(
                out=neg_b1[:], in0=bias_sb[:, :, 0:8], scalar1=-1.0, scalar2=None, op0=ALU.mult
            )
            nc.vector.tensor_tensor(
                out=delta[:], in0=bias_sb[:, :, 8:16], in1=bias_sb[:, :, 0:8], op=ALU.subtract
            )

        x_codes = codes.tile([P, 2, B], U32, name="x_codes", align_bytes=64)
        x_scales = codes.tile([P, 2, B], U8, name="x_scales", align_bytes=64)
        w_codes = {}
        w_scales = {}
        for J in range(N_J):
            for h in range(2):
                w_codes[(J, h)] = codes.tile([P, 512], U32, name="wc%d_%d" % (J, h), align_bytes=64)
                w_scales[(J, h)] = codes.tile([P, 512], U8, name="ws%d_%d" % (J, h), align_bytes=64)
        wide_codes = {}
        wide_scales = {}
        for D in range(N_D):
            for h in range(2):
                wide_codes[(D, h)] = codes.tile(
                    [P, 2, 512], U32, name="vc%d_%d" % (D, h), align_bytes=64
                )
                wide_scales[(D, h)] = codes.tile(
                    [P, 2, 512], U8, name="vs%d_%d" % (D, h), align_bytes=64
                )

        def copy_out(engine, dst, src):
            if engine == "vector":
                nc.vector.tensor_copy(out=dst, in_=src)
            else:
                nc.scalar.copy(out=dst, in_=src)

        x_compact = {}
        x_grouped = {}

        def x_compaction(bb, engine):
            t = stage.tile([P, K], BF16, name="xcmp", tag="xcmp", bufs=4)
            src = x_in[bb].rearrange("p (k two) -> p k two", two=2)[:, :, 1]
            if engine == "vector":
                nc.vector.tensor_copy(out=t[:], in_=src)
            else:
                nc.gpsimd.tensor_scalar(
                    out=t[:], in0=src, scalar1=1.0, scalar2=0.0,
                    op0=ALU.mult, op1=ALU.add,
                )
            x_compact[bb] = t

        def x_transposes(bb, engine="scalar"):
            words = x_compact[bb][:].bitcast(F32)
            bank = next_bank()
            for q in range(4):
                nc.tensor.transpose(
                    bank[:, q * P : (q + 1) * P], words[:, q * P : (q + 1) * P], ident[:]
                )
            g_tile = stage.tile([P, K], BF16, name="xg", tag="xg", align_bytes=64)
            copy_out(
                engine,
                g_tile[:].bitcast(F32).rearrange("p (g b u) -> p g b u", g=2, u=2),
                bank[:].rearrange("p (g u b) -> p g b u", g=2, u=2),
            )
            x_grouped[bb] = g_tile

        def x_quantise(bb):
            for g in range(2):
                nc.vector.quantize_mx(
                    out=x_codes[:, g, bb * P : (bb + 1) * P].bitcast(FP8X4),
                    scales=x_scales[:, g, bb * P : (bb + 1) * P],
                    in_=x_grouped[bb][:, g * 512 : (g + 1) * 512],
                )

        w_grouped = {}

        def w_transposes(unit, s, engine="scalar"):
            words = w_in[unit][:, s, :].bitcast(F32)
            g_tile = stage.tile([P, K], BF16, name="wg", tag="wg", bufs=WG_BUFS, align_bytes=64)
            bank = next_bank()
            for q in range(4):
                nc.tensor.transpose(bank[:, q * P : (q + 1) * P], words[:, q * P : (q + 1) * P], ident[:])
            copy_out(
                engine,
                g_tile[:].bitcast(F32).rearrange("p (g n u) -> p g n u", g=2, u=2),
                bank[:].rearrange("p (g u n) -> p g n u", g=2, u=2),
            )
            w_grouped[(unit, s)] = g_tile

        def w_quantise(unit, s):
            if unit[0] == "R":
                key = (unit[1], unit[2])
                nc.vector.quantize_mx(
                    out=w_codes[key][:, s * 256 : (s + 1) * 256].bitcast(FP8X4),
                    scales=w_scales[key][:, s * 256 : (s + 1) * 256],
                    in_=w_grouped[(unit, s)][:],
                )
            else:
                key = (unit[1], unit[2])
                lo = unit[3] * 256 + s * P
                for g in range(2):
                    nc.vector.quantize_mx(
                        out=wide_codes[key][:, g, lo : lo + P].bitcast(FP8X4),
                        scales=wide_scales[key][:, g, lo : lo + P],
                        in_=w_grouped[(unit, s)][:, g * 512 : (g + 1) * 512],
                    )

        def quantise(job):
            if job[0] == "x":
                x_quantise(job[1])
            else:
                w_quantise(job[1], job[2])

        def mx(J, c, s, h):
            acc = next_bank()
            for g in range(2):
                lo = s * 256 + g * P
                nc.tensor.matmul_mx(
                    out=acc[:],
                    lhsT=w_codes[(J, h)][:, lo : lo + P].bitcast(FP8X4),
                    lhsT_scale=w_scales[(J, h)][:, lo : lo + P],
                    rhs=x_codes[:, g, c * 512 : (c + 1) * 512].bitcast(FP8X4),
                    rhs_scale=x_scales[:, g, c * 512 : (c + 1) * 512],
                    start=(g == 0),
                    stop=(g == 1),
                )
            return acc

        def fold_first(J, s, acc):
            d2 = epi.tile([P, 512], F32, name="d2", tag="d2")
            nc.vector.tensor_scalar(
                out=d2[:], in0=acc[:],
                scalar1=delta[:, s, J : J + 1], scalar2=neg_b1[:, s, J : J + 1],
                op0=ALU.add, op1=ALU.max,
            )
            return d2

        def fold_second(J, s, acc, d2):
            r = epi.tile([P, 512], F32, name="r", tag="r")
            nc.vector.scalar_tensor_tensor(
                out=r[:], in0=acc[:], scalar=neg_b1[:, s, J : J + 1], in1=d2[:],
                op0=ALU.max, op1=ALU.subtract,
            )
            return r

        def mx_wide(D, bb, h):
            acc = next_bank()
            for g in range(2):
                nc.tensor.matmul_mx(
                    out=acc[:],
                    lhsT=x_codes[:, g, bb * P : (bb + 1) * P].bitcast(FP8X4),
                    lhsT_scale=x_scales[:, g, bb * P : (bb + 1) * P],
                    rhs=wide_codes[(D, h)][:, g, :].bitcast(FP8X4),
                    rhs_scale=wide_scales[(D, h)][:, g, :],
                    start=(g == 0),
                    stop=(g == 1),
                )
            return acc

        def add_bias(D, h, acc):
            t = epi.tile([P, 512], F32, name="t", tag="t", bufs=T_BUFS)
            nc.vector.tensor_tensor(
                out=t[:], in0=acc[:], in1=bias_wide[:, h, D * 512 : (D + 1) * 512], op=ALU.add
            )
            return t

        def relu(t, engine):
            if engine == "scalar":
                nc.scalar.activation(out=t[:], in_=t[:], func=mybir.ActivationFunctionType.Relu)
            else:
                nc.gpsimd.tensor_scalar(
                    out=t[:], in0=t[:], scalar1=3.0e38, scalar2=0.0, op0=ALU.min, op1=ALU.max
                )

        wide_count = [0]

        def subtract_and_store(D, bb, t1, t2):
            o = wide_out[wide_count[0] % 4]
            wide_count[0] += 1
            nc.gpsimd.tensor_tensor(out=o[:, :, 0], in0=t1[:], in1=t2[:], op=ALU.subtract)
            lo = 2 * (J_SPLIT + D * 512)
            nc.sync.dma_start(
                out=out2d[bb * P : (bb + 1) * P, lo : lo + 1024],
                in_=o[:].rearrange("p j e -> p (j e)"),
            )

        def r_transposes(r_tiles):
            for bb in range(4):
                for s in range(2):
                    nc.tensor.transpose(
                        r_bank[bb][:, s * P : (s + 1) * P],
                        r_tiles[s][:, bb * P : (bb + 1) * P],
                        ident[:],
                    )

        def copy_out_and_store(J, c, vector_blocks, split_store):
            o = io.tile([P, 4, 512], F32, name="o", tag="io")
            for bb in range(4):
                copy_out(
                    "vector" if bb in vector_blocks else "scalar",
                    o[:, bb, :].rearrange("p (n s e) -> p n s e", s=2, e=2),
                    r_bank[bb][:].rearrange("p (e s n) -> p n s e", e=2, s=2),
                )
                if split_store:
                    nc.sync.dma_start(
                        out=out_view[c][:, bb, J * 512 : (J + 1) * 512], in_=o[:, bb, :]
                    )
            if not split_store:
                nc.sync.dma_start(out=out_view[c][:, :, J * 512 : (J + 1) * 512], in_=o[:])

        x_compaction(0, "vector")
        x_transposes(0)
        x_compaction(1, "vector")
        x_transposes(1)
        x_compaction(2, "vector")
        x_quantise(0)
        x_transposes(2)
        x_compaction(3, "vector")
        x_quantise(1)
        x_transposes(3)
        x_quantise(2)
        bias_scalars()
        head_w = [(unit, s) for unit in units[0:2] for s in range(2)]
        for i, (unit, s) in enumerate(head_w):
            w_transposes(unit, s, HEAD_ENGINES[i])
            if i == 0:
                x_quantise(3)
            if i >= 1:
                w_quantise(*head_w[i - 1])
        w_quantise(*head_w[3])
        for bb in range(4, 8):
            x_compaction(bb, "gpsimd")

        items = [
            ("R", 0, 0), ("R", 1, 0), ("R", 2, 0), ("R", 3, 0),
            ("B", 0, (0, 1)), ("B", 0, (2, 3)), ("R", 0, 1),
            ("B", 0, (4, 5)), ("B", 0, (6, 7)), ("R", 1, 1),
            ("B", 1, (0, 1)), ("B", 1, (2, 3)), ("R", 2, 1),
            ("B", 1, (4, 5)), ("B", 1, (6, 7)), ("R", 3, 1),
        ]
        n_items = len(items)
        w_after = {0: units[2:6], 1: units[6:10], 2: units[10:14], 3: units[14:16]}
        x_after = {3: [4, 5, 6, 7]}

        jobs = []
        to_transpose = None
        to_copy = None
        for i, item in enumerate(items):
            last = i == n_items - 1
            if to_copy is not None:
                copy_out_and_store(to_copy[0], to_copy[1], vector_blocks=(), split_store=False)
                to_copy = None
            fresh = None
            if item[0] == "R":
                J, c = item[1], item[2]
                acc = {}
                for h in (1, 0):
                    for s in range(2):
                        acc[(s, h)] = mx(J, c, s, h)
                d20 = fold_first(J, 0, acc[(0, 1)])
                d21 = fold_first(J, 1, acc[(1, 1)])
                r0 = fold_second(J, 0, acc[(0, 0)], d20)
                r1 = fold_second(J, 1, acc[(1, 0)], d21)
                fresh = (J, c, [r0, r1])
            else:
                D = item[1]
                acc = {}
                for bb in item[2]:
                    for h in (1, 0):
                        acc[(bb, h)] = mx_wide(D, bb, h)
                sums = {}
                for bb in item[2]:
                    for h in (1, 0):
                        sums[(bb, h)] = add_bias(D, h, acc[(bb, h)])
                for bb in item[2]:
                    relu(sums[(bb, 1)], RELU_ENGINES[0])
                    relu(sums[(bb, 0)], RELU_ENGINES[1])
                    subtract_and_store(D, bb, sums[(bb, 0)], sums[(bb, 1)])
            for job in jobs:
                quantise(job)
            jobs = []
            for k, unit in enumerate(w_after.get(i, [])):
                for s in range(2):
                    w_transposes(unit, s, "vector" if (2 * k + s) % V_COPY_EVERY == 1 else "scalar")
                    jobs.append(("w", unit, s))
            for bb in x_after.get(i, []):
                x_transposes(bb)
                jobs.append(("x", bb))
            if i in EARLY_JOBS:
                for job in jobs:
                    quantise(job)
                jobs = []
            if to_transpose is not None:
                r_transposes(to_transpose[2])
                to_copy = (to_transpose[0], to_transpose[1])
                to_transpose = None
            if fresh is not None:
                to_transpose = fresh
        r_transposes(to_transpose[2])
        copy_out_and_store(to_transpose[0], to_transpose[1], vector_blocks=(1, 3), split_store=True)
